import numpy as np
import ml_dtypes


def mxq(x, axis, fmt="e4m3"):
    dtype, down = {"e4m3": (ml_dtypes.float8_e4m3fn, 7), "e5m2": (ml_dtypes.float8_e5m2, 14)}[fmt]
    v = np.moveaxis(np.asarray(x, np.float32).astype(ml_dtypes.bfloat16).astype(np.float64), axis, -1)
    blocks = v.reshape(v.shape[:-1] + (-1, 32))
    amax = np.abs(blocks).max(-1, keepdims=True)
    byte = np.maximum(np.where(amax > 0, np.frexp(amax)[1] - 1 + 127, 0) - down, 1)
    scale = np.exp2(byte - 127.0)
    codes = (blocks / scale).astype(np.float32).astype(dtype).astype(np.float64)
    return np.moveaxis((codes * scale).reshape(v.shape), -1, axis)


WIDE = False


def mx_kscale(k):
    if not WIDE:
        return np.ones(k)
    levels = np.array([10, -10, 5, -5, 0])
    if k % 512:
        return np.exp2(np.random.permutation(np.resize(levels, k // 32))).repeat(32)
    a = np.empty((k // 512, 16))
    for p in range(k // 512):
        a[p, :8] = np.random.permutation(np.resize(levels, 8))
        for g in range(8):
            far = levels[np.abs(levels - a[p, g]) >= 10]
            a[p, g + 8] = far[np.random.randint(len(far))]
    return np.exp2(a.ravel()).repeat(32)


BF16 = ml_dtypes.bfloat16


def bf(x):
    return np.asarray(x, np.float32).astype(BF16)


def f64(x):
    return np.asarray(x).astype(np.float64)


B, T, C, H, G, D = 2, 512, 1024, 8, 2, 128
EPS = 1e-6


def rmsnorm(v, w):
    return v / np.sqrt(np.mean(v * v, axis=-1, keepdims=True) + EPS) * w


def apply_rotary(v, cos, sin):
    v1, v2 = np.split(v, 2, axis=-1)
    return np.concatenate([v1 * cos - v2 * sin, v1 * sin + v2 * cos], axis=-1)


def draw0():
    s = mx_kscale(C)
    ang = np.arange(T)[:, None] / 10000.0 ** (np.arange(0, D, 2) / D)[None, :]
    a = 4.0 * np.sqrt(EPS / C)
    return {"x": bf(np.random.standard_normal((B, T, C)) * s),
            "cos": bf(np.cos(ang)[None, None, :, :]),
            "sin": bf(np.sin(ang)[None, None, :, :]),
            "wq": bf(np.random.standard_normal((G * H * D, C)) * a / s[None, :]),
            "wk": bf(np.random.standard_normal((H * D, C)) * a / s[None, :]),
            "wv": bf(np.random.standard_normal((H * D, C)) / np.sqrt(C) / s[None, :]),
            "q_norm_w": bf(1.0 + 0.1 * np.random.standard_normal(D)),
            "k_norm_w": bf(1.0 + 0.1 * np.random.standard_normal(D))}


def core(x, cos, sin, wq, wk, wv, q_norm_w, k_norm_w):
    xq = mxq(f64(x), 2, "e4m3")
    q = (xq @ mxq(f64(wq), 1, "e4m3").T).reshape(B, T, G * H, D).transpose(0, 2, 1, 3)
    k = (xq @ mxq(f64(wk), 1, "e4m3").T).reshape(B, T, H, D).transpose(0, 2, 1, 3)
    v = (xq @ mxq(f64(wv), 1, "e4m3").T).reshape(B, T, H, D).transpose(0, 2, 1, 3)
    q = rmsnorm(q, f64(q_norm_w))
    k = rmsnorm(k, f64(k_norm_w))
    c, sn = f64(cos)[:, :, :T, :], f64(sin)[:, :, :T, :]
    q = apply_rotary(q, c, sn)
    k = apply_rotary(k, c, sn)
    return q, k, v


def e4m3fn_bytes(y):
    return np.clip(np.asarray(y, np.float64), -448.0, 448.0).astype(np.float32).astype(ml_dtypes.float8_e4m3fn).view(np.uint8)


def e4m3fn_values(b):
    return np.asarray(b, np.uint8).view(ml_dtypes.float8_e4m3fn).astype(np.float64)


def setup_inputs():
    d = draw0()
    x0 = np.asarray(d['wq']).astype(np.float64)
    s = (np.max(np.abs(x0), axis=(0,), keepdims=True) / 448.0).astype(np.float32)
    out = {}
    for k, v in d.items():
        if k == 'wq':
            out['wq_bytes'] = e4m3fn_bytes(x0 / s.astype(np.float64))
            out['wq_scale'] = s
        else:
            out[k] = v
    return out


def reference(x, cos, sin, wq_bytes, wq_scale, wk, wv, q_norm_w, k_norm_w):
    return core(x, cos, sin, e4m3fn_values(wq_bytes) * wq_scale.astype(np.float64), wk, wv, q_norm_w, k_norm_w)

@@ -1,0 +1,337 @@
+from contextlib import ExitStack
+
+import concourse.mybir as mybir
+from concourse.masks import make_identity
+
+F32 = mybir.dt.float32
+BF16 = mybir.dt.bfloat16
+U32 = mybir.dt.uint32
+U8 = mybir.dt.uint8
+FP8 = mybir.dt.float8_e4m3fn
+FP8X4 = mybir.dt.float8_e4m3fn_x4
+ALU = mybir.AluOpType
+ACT = mybir.ActivationFunctionType
+
+P = 128
+BATCH, SEQ, K = 2, 512, 1024
+D = 128
+HALF = D // 2
+EPS = 1e-6
+N_TILE = 512
+HEADS = N_TILE // D
+TOK = SEQ // P
+PASSES = K // 512
+Q_TILES, K_TILES, V_TILES = 4, 2, 2
+LOOK = 6
+
+FLOPS = 2 * BATCH * SEQ * K * (Q_TILES + K_TILES + V_TILES) * N_TILE
+
+
+def tile_qwen3attention_pa_kernel(
+    tc, x, cos, sin, wq_bytes, wq_scale, wk, wv, q_norm_w, k_norm_w, out_0, out_1, out_2
+):
+    nc = tc.nc
+    outs = {"q": out_0, "k": out_1, "v": out_2}
+    groups = [("q", n, b) for n in range(Q_TILES) for b in range(BATCH)] + [
+        ("k", n, b) for n in range(K_TILES) for b in range(BATCH)
+    ]
+    n_banks = len(groups) * TOK
+    late_sets = [("q", 2), ("q", 3), ("k", 0), ("k", 1)]
+    quantize_at = {3: (("v", 1), None), 7: (("q", 2), None)}
+    for s in (1, 2, 3):
+        quantize_at[8 * s + 3] = (late_sets[s], 0)
+        quantize_at[8 * s + 7] = (late_sets[s], 1)
+    side_slots = [i for i in range(40) if i % 5 != 4]
+    side_jobs = dict((side_slots[u], u) for u in range(len(side_slots)))
+
+    with ExitStack() as ctx:
+        ctx.enter_context(tc.manual_schedule())
+        keep = ctx.enter_context(tc.tile_pool(name="keep", bufs=1))
+        small = ctx.enter_context(tc.tile_pool(name="small", bufs=8))
+        late = ctx.enter_context(tc.tile_pool(name="late", bufs=1))
+        ps_o = ctx.enter_context(tc.psum_pool(name="ps_o", bufs=4))
+        pools = {}
+
+        zero = keep.tile([P, 1], F32, name="zero")
+        nc.vector.memset(zero[:], 0.0)
+        eps_t = keep.tile([P, 1], F32, name="eps_t")
+        nc.vector.tensor_scalar(out=eps_t[:], in0=zero[:], scalar1=EPS, scalar2=None, op0=ALU.add)
+        ident = keep.tile([P, P], F32, name="ident")
+        make_identity(nc, ident[:])
+        warm = keep.tile([P, 1], F32, name="warm")
+        nc.scalar.activation(out=warm[:], in_=eps_t[:], func=ACT.Abs_reciprocal_sqrt)
+
+        cs = keep.tile([P, TOK, HALF], BF16, name="cs")
+        nc.sync.dma_start(out=cs[:], in_=cos[0, 0].rearrange("(p j) f -> p j f", j=TOK))
+        sn = keep.tile([P, TOK, HALF], BF16, name="sn")
+        nc.sync.dma_start(out=sn[:], in_=sin[0, 0].rearrange("(p j) f -> p j f", j=TOK))
+        gain_q = keep.tile([P, D], BF16, name="gain_q")
+        nc.sync.dma_start(out=gain_q[:], in_=q_norm_w.partition_broadcast(P))
+        gain_k = keep.tile([P, D], BF16, name="gain_k")
+        nc.sync.dma_start(out=gain_k[:], in_=k_norm_w.partition_broadcast(P))
+
+        codes = {}
+        planes = {}
+        for key in [("x", b) for b in range(BATCH)] + [
+            (kind, n)
+            for kind, tiles in (("q", Q_TILES), ("k", K_TILES), ("v", V_TILES))
+            for n in range(tiles)
+        ]:
+            codes[key] = keep.tile([P, PASSES * N_TILE], U32, name="codes_%s%d" % key, align_bytes=64)
+            planes[key] = keep.tile([P, PASSES * N_TILE], U8, name="planes_%s%d" % key, align_bytes=64)
+
+        tables = {}
+        raw = {}
+        grouped = {}
+        banks = {}
+        rstd = {}
+        state = {}
+
+        def make_table(kind, gain):
+            tab = keep.tile([P, TOK, 2 * D], F32, name="tab_%s" % kind)
+            tv = tab[:].rearrange("p j (a c f) -> p j a c f", a=2, c=2)
+            w1 = gain[:, 0:HALF].unsqueeze(1).to_broadcast([P, TOK, HALF])
+            w2 = gain[:, HALF:D].unsqueeze(1).to_broadcast([P, TOK, HALF])
+            nc.vector.tensor_tensor(out=tv[:, :, 0, 0, :], in0=cs[:], in1=w1, op=ALU.mult)
+            nc.vector.scalar_tensor_tensor(
+                out=tv[:, :, 0, 1, :], in0=sn[:], scalar=-1.0, in1=w2, op0=ALU.mult, op1=ALU.mult
+            )
+            nc.vector.tensor_tensor(out=tv[:, :, 1, 0, :], in0=sn[:], in1=w1, op=ALU.mult)
+            nc.vector.tensor_tensor(out=tv[:, :, 1, 1, :], in0=cs[:], in1=w2, op=ALU.mult)
+            tables[kind] = tab
+
+        def turn_bank(key, i, psum):
+            if i == 0:
+                wg = late.tile([P, PASSES * N_TILE * 4], BF16, name="wg", bufs=4, align_bytes=64)
+                grouped[key] = wg
+            dst = grouped[key][:].bitcast(F32).rearrange("p (g c u) -> p g c u", g=PASSES, u=2)
+            words = raw[key][:, i, :].bitcast(F32)
+            tb = psum.tile([P, N_TILE], F32, name="tb")
+            for g in range(PASSES):
+                for u in range(2):
+                    q = 2 * g + u
+                    nc.tensor.transpose(
+                        tb[:, q * P : (q + 1) * P], words[:, 256 * g + u : 256 * (g + 1) : 2], ident[:]
+                    )
+            nc.scalar.copy(
+                out=dst[:, :, i * P : (i + 1) * P, :],
+                in_=tb[:].rearrange("p (g u r) -> p g r u", g=PASSES, u=2),
+            )
+
+        def quantize(key, g=None):
+            cols = slice(0, PASSES * N_TILE) if g is None else slice(g * N_TILE, (g + 1) * N_TILE)
+            nc.vector.quantize_mx(
+                out=codes[key][:, cols].bitcast(FP8X4),
+                scales=planes[key][:, cols],
+                in_=grouped[key][:, 4 * cols.start : 4 * cols.stop],
+            )
+
+        def mx_bank(bank, wkey, b, j):
+            for g in range(PASSES):
+                m_cols = slice(g * N_TILE + j * P, g * N_TILE + (j + 1) * P)
+                n_cols = slice(g * N_TILE, (g + 1) * N_TILE)
+                nc.tensor.matmul_mx(
+                    out=bank[:],
+                    lhsT=codes[("x", b)][:, m_cols].bitcast(FP8X4),
+                    lhsT_scale=planes[("x", b)][:, m_cols],
+                    rhs=codes[wkey][:, n_cols].bitcast(FP8X4),
+                    rhs_scale=planes[wkey][:, n_cols],
+                    start=(g == 0),
+                    stop=(g == PASSES - 1),
+                )
+
+        def fill(i):
+            kind, n, b = groups[i // TOK]
+            if i % LOOK < 4:
+                ob = ps_o.tile([P, N_TILE], F32, name="ob")
+            else:
+                ob = pools["ps_o2"].tile([P, N_TILE], F32, name="ob2")
+            mx_bank(ob, (kind, n), b, i % TOK)
+            banks[i] = ob
+            odd = i % 2
+            if odd == 0:
+                ss = small.tile([P, 2 * HEADS], F32, name="ss")
+                state["ss"] = ss
+            ss = state["ss"]
+            for h in range(HEADS):
+                junk = small.tile([P, D], BF16, name="junk")
+                col = odd * HEADS + h
+                nc.scalar.activation(
+                    out=junk[:], in_=ob[:, h * D : (h + 1) * D], func=ACT.Square, accum_out=ss[:, col : col + 1]
+                )
+            if odd == 1:
+                rr = small.tile([P, 2 * HEADS], F32, name="rr")
+                nc.scalar.activation(
+                    out=rr[:], in_=ss[:], func=ACT.Abs_reciprocal_sqrt, bias=eps_t[:, 0:1], scale=1.0 / D
+                )
+                rstd[i - 1] = rr
+                rstd[i] = rr
+
+        with tc.psum_pool(name="ps_t", bufs=4) as ps_t, tc.tile_pool(name="stage", bufs=1) as stage:
+            scale_bc = stage.tile([P, K], F32, name="scale_bc")
+            nc.sync.dma_start(out=scale_bc[:], in_=wq_scale.rearrange("o k -> (o k)").partition_broadcast(P))
+            wq_in = {}
+
+            def load_bytes(n, pieces):
+                wq_codes_in = stage.tile([P, HEADS, K], U8, name="wq_codes_in%d" % n)
+                rows = wq_bytes[n * N_TILE : (n + 1) * N_TILE, :].rearrange("(i r) k -> r i k", r=P)
+                step = HEADS // pieces
+                for i in range(0, HEADS, step):
+                    nc.sync.dma_start(out=wq_codes_in[:, i : i + step, :], in_=rows[:, i : i + step, :])
+                wq_in[n] = wq_codes_in
+
+            def load_x(b):
+                t = stage.tile([P, TOK, K], BF16, name="raw_x%d" % b)
+                nc.sync.dma_start(out=t[:], in_=x[b].rearrange("(p j) k -> p j k", j=TOK))
+                raw[("x", b)] = t
+
+            def load_w(kind, w, n):
+                pool = late if (kind, n) in late_sets else stage
+                t = pool.tile([P, HEADS, K], BF16, name="raw_%s%d" % (kind, n))
+                nc.sync.dma_start(out=t[:], in_=w[n * N_TILE : (n + 1) * N_TILE, :].rearrange("(i r) k -> r i k", r=P))
+                raw[(kind, n)] = t
+
+            def widen(n):
+                if ("q", n) in late_sets:
+                    wide = late.tile([P, HEADS, K], BF16, name="wide%d" % n)
+                else:
+                    wide = stage.tile([P, HEADS, K], BF16, name="wide%d" % n)
+                for i in range(HEADS):
+                    nc.vector.tensor_tensor(
+                        out=wide[:, i, :], in0=wq_in[n][:, i, :].bitcast(FP8), in1=scale_bc[:], op=ALU.mult
+                    )
+                raw[("q", n)] = wide
+
+            def turn(key):
+                for i in range(HEADS):
+                    turn_bank(key, i, ps_t)
+
+            load_bytes(0, 2)
+            load_x(0)
+            load_bytes(1, 1)
+            load_x(1)
+            load_w("v", wv, 0)
+            load_bytes(2, 1)
+            load_w("v", wv, 1)
+            load_bytes(3, 1)
+            load_w("k", wk, 0)
+            load_w("k", wk, 1)
+
+            make_table("q", gain_q)
+            make_table("k", gain_k)
+            widen(0)
+            turn(("x", 0))
+            turn(("q", 0))
+            widen(1)
+            quantize(("x", 0))
+            widen(2)
+            turn(("x", 1))
+            turn(("q", 1))
+            turn(("v", 0))
+            quantize(("q", 0))
+            for i in range(4):
+                fill(i)
+            turn(("v", 1))
+            quantize(("x", 1))
+            widen(3)
+            quantize(("q", 1))
+            quantize(("v", 0))
+
+        pools["ps_o2"] = ctx.enter_context(tc.psum_pool(name="ps_o2", bufs=LOOK - 4))
+        ps_s = ctx.enter_context(tc.psum_pool(name="ps_s", bufs=2))
+        zpool = ctx.enter_context(tc.tile_pool(name="zpool", bufs=3))
+        opool = ctx.enter_context(tc.tile_pool(name="opool", bufs=3))
+
+        def dram_group(kind, n, b):
+            return outs[kind][b, n * HEADS : (n + 1) * HEADS]
+
+        def rotate(i, zt, h):
+            kind = groups[i // TOK][0]
+            j = i % TOK
+            col = (i % 2) * HEADS + h
+            nc.vector.scalar_tensor_tensor(
+                out=zt[:, h, j, :].rearrange("p (a d) -> p a d", a=2),
+                in0=banks[i][:, h * D : (h + 1) * D].unsqueeze(1).to_broadcast([P, 2, D]),
+                scalar=rstd[i][:, col : col + 1],
+                in1=tables[kind][:, j, :].rearrange("p (a d) -> p a d", a=2),
+                op0=ALU.mult,
+                op1=ALU.mult,
+            )
+
+        def v_bank(k):
+            n, b, j = k // (BATCH * TOK), (k // TOK) % BATCH, k % TOK
+            vb = ps_s.tile([P, N_TILE], F32, name="tb")
+            mx_bank(vb, ("v", n), b, j)
+            if j == 0:
+                ov = opool.tile([P, HEADS, TOK, D], F32, name="ov", bufs=2)
+                state["ov"] = ov
+            ov = state["ov"]
+            nc.scalar.copy(out=ov[:, :, j, :], in_=vb[:].rearrange("p (h d) -> p h d", h=HEADS))
+            if j == TOK - 1:
+                nc.sync.dma_start(
+                    out=dram_group("v", n, b).rearrange("h (p j) d -> p h (j d)", j=TOK),
+                    in_=ov[:].rearrange("p h j d -> p h (j d)"),
+                )
+
+        for i in range(4, LOOK):
+            fill(i)
+        zt = None
+        ot = None
+        for i in range(n_banks):
+            gi, j = divmod(i, TOK)
+            kind, n, b = groups[gi]
+            if j == 0:
+                zt = zpool.tile([P, HEADS, TOK, 2 * D], F32, name="zt")
+                ot = opool.tile([P, HEADS, TOK, D], F32, name="ot")
+            for h in range(HEADS - 1):
+                rotate(i, zt, h)
+            if i in quantize_at:
+                quantize(quantize_at[i][0], quantize_at[i][1])
+            rotate(i, zt, HEADS - 1)
+            if i + LOOK < n_banks:
+                fill(i + LOOK)
+            if i in side_jobs:
+                u = side_jobs[i]
+                if u < HEADS * len(late_sets):
+                    turn_bank(late_sets[u // HEADS], u % HEADS, ps_s)
+                else:
+                    v_bank(u - HEADS * len(late_sets))
+            if gi == len(groups) - 1:
+                if j == TOK - 1:
+                    for jj in range(TOK):
+                        zv = zt[:, :, jj, :].rearrange("p h (a c f) -> p h a c f", a=2, c=2)
+                        nc.vector.tensor_tensor(
+                            out=ot[:, :, jj, :].rearrange("p h (a f) -> p h a f", a=2),
+                            in0=zv[:, :, :, 0, :],
+                            in1=zv[:, :, :, 1, :],
+                            op=ALU.add,
+                        )
+                        nc.scalar.dma_start(
+                            out=dram_group(kind, n, b).rearrange("h (p j) d -> p h j d", j=TOK)[:, :, jj, :],
+                            in_=ot[:, :, jj, :],
+                        )
+            elif gi == len(groups) - 2:
+                if j % 2 == 1:
+                    zv = zt[:, :, j - 1 : j + 1, :].rearrange("p h j (a c f) -> p h j a c f", a=2, c=2)
+                    nc.gpsimd.tensor_tensor(
+                        out=ot[:, :, j - 1 : j + 1, :].rearrange("p h j (a f) -> p h j a f", a=2),
+                        in0=zv[:, :, :, :, 0, :],
+                        in1=zv[:, :, :, :, 1, :],
+                        op=ALU.add,
+                    )
+                    nc.sync.dma_start(
+                        out=dram_group(kind, n, b).rearrange("h (p j) d -> p h j d", j=TOK)[:, :, j - 1 : j + 1, :],
+                        in_=ot[:, :, j - 1 : j + 1, :],
+                    )
+            elif j == TOK - 1:
+                zv = zt[:].rearrange("p h j (a c f) -> p (h j) a c f", a=2, c=2)
+                nc.gpsimd.tensor_tensor(
+                    out=ot[:].rearrange("p h j (a f) -> p (h j) a f", a=2),
+                    in0=zv[:, :, :, 0, :],
+                    in1=zv[:, :, :, 1, :],
+                    op=ALU.add,
+                )
+                nc.sync.dma_start(
+                    out=dram_group(kind, n, b).rearrange("h (p j) d -> p h (j d)", j=TOK),
+                    in_=ot[:].rearrange("p h j d -> p h (j d)"),
+                )

@@ -277,7 +277,7 @@ def tile_qwen3attention_pa_kernel(
             fill(i)
         zt = None
         ot = None
-        for i in range(n_banks):
+        for i in range(n_banks - TOK):
             gi, j = divmod(i, TOK)
             kind, n, b = groups[gi]
             if j == 0:
@@ -296,21 +296,7 @@ def tile_qwen3attention_pa_kernel(
                     turn_bank(late_sets[u // HEADS], u % HEADS, ps_s)
                 else:
                     v_bank(u - HEADS * len(late_sets))
-            if gi == len(groups) - 1:
-                if j == TOK - 1:
-                    for jj in range(TOK):
-                        zv = zt[:, :, jj, :].rearrange("p h (a c f) -> p h a c f", a=2, c=2)
-                        nc.vector.tensor_tensor(
-                            out=ot[:, :, jj, :].rearrange("p h (a f) -> p h a f", a=2),
-                            in0=zv[:, :, :, 0, :],
-                            in1=zv[:, :, :, 1, :],
-                            op=ALU.add,
-                        )
-                        nc.scalar.dma_start(
-                            out=dram_group(kind, n, b).rearrange("h (p j) d -> p h j d", j=TOK)[:, :, jj, :],
-                            in_=ot[:, :, jj, :],
-                        )
-            elif gi == len(groups) - 2:
+            if gi == len(groups) - 2:
                 if j % 2 == 1:
                     zv = zt[:, :, j - 1 : j + 1, :].rearrange("p h j (a c f) -> p h j a c f", a=2, c=2)
                     nc.gpsimd.tensor_tensor(
@@ -335,3 +321,29 @@ def tile_qwen3attention_pa_kernel(
                     out=dram_group(kind, n, b).rearrange("h (p j) d -> p h (j d)", j=TOK),
                     in_=ot[:].rearrange("p h j d -> p h (j d)"),
                 )
+
+        kind, n, b = groups[-1]
+        first = n_banks - TOK
+        zt = zpool.tile([P, HEADS, TOK, 2 * D], F32, name="zt")
+        ot = opool.tile([P, HEADS, TOK, D], F32, name="ot")
+
+        def add_head(h):
+            zv = zt[:, h, :, :].rearrange("p j (a c f) -> p j a c f", a=2, c=2)
+            nc.vector.tensor_tensor(
+                out=ot[:, h, :, :].rearrange("p j (a f) -> p j a f", a=2),
+                in0=zv[:, :, :, 0, :],
+                in1=zv[:, :, :, 1, :],
+                op=ALU.add,
+            )
+            nc.scalar.dma_start(
+                out=dram_group(kind, n, b)[h].rearrange("(p j) d -> p (j d)", j=TOK),
+                in_=ot[:, h, :, :].rearrange("p j d -> p (j d)"),
+            )
+
+        for h in range(HEADS):
+            for jj in range(TOK):
+                rotate(first + jj, zt, h)
+            if h == HEADS - 2:
+                add_head(0)
+        for h in range(1, HEADS):
+            add_head(h)

@@ -100,7 +100,7 @@ def tile_qwen3attention_pa_kernel(
             nc.vector.tensor_tensor(out=tv[:, :, 1, 1, :], in0=cs[:], in1=w2, op=ALU.mult)
             tables[kind] = tab
 
-        def turn_bank(key, i, psum):
+        def turn_bank(key, i, psum, on_vector=False):
             if i == 0:
                 wg = late.tile([P, PASSES * N_TILE * 4], BF16, name="wg", bufs=4, align_bytes=64)
                 grouped[key] = wg
@@ -113,7 +113,8 @@ def tile_qwen3attention_pa_kernel(
                     nc.tensor.transpose(
                         tb[:, q * P : (q + 1) * P], words[:, 256 * g + u : 256 * (g + 1) : 2], ident[:]
                     )
-            nc.scalar.copy(
+            copy = nc.vector.tensor_copy if on_vector else nc.scalar.copy
+            return lambda: copy(
                 out=dst[:, :, i * P : (i + 1) * P, :],
                 in_=tb[:].rearrange("p (g u r) -> p g r u", g=PASSES, u=2),
             )
@@ -204,7 +205,7 @@ def tile_qwen3attention_pa_kernel(
 
             def turn(key):
                 for i in range(HEADS):
-                    turn_bank(key, i, ps_t)
+                    turn_bank(key, i, ps_t)()
 
             load_bytes(0, 2)
             load_x(0)
@@ -258,7 +259,7 @@ def tile_qwen3attention_pa_kernel(
                 op1=ALU.mult,
             )
 
-        def v_bank(k):
+        def v_bank(k, on_vector):
             n, b, j = k // (BATCH * TOK), (k // TOK) % BATCH, k % TOK
             vb = ps_s.tile([P, N_TILE], F32, name="tb")
             mx_bank(vb, ("v", n), b, j)
@@ -266,36 +267,48 @@ def tile_qwen3attention_pa_kernel(
                 ov = opool.tile([P, HEADS, TOK, D], F32, name="ov", bufs=2)
                 state["ov"] = ov
             ov = state["ov"]
-            nc.scalar.copy(out=ov[:, :, j, :], in_=vb[:].rearrange("p (h d) -> p h d", h=HEADS))
-            if j == TOK - 1:
-                nc.sync.dma_start(
-                    out=dram_group("v", n, b).rearrange("h (p j) d -> p h (j d)", j=TOK),
-                    in_=ov[:].rearrange("p h j d -> p h (j d)"),
-                )
+            copy = nc.vector.tensor_copy if on_vector else nc.scalar.copy
+
+            def empty():
+                copy(out=ov[:, :, j, :], in_=vb[:].rearrange("p (h d) -> p h d", h=HEADS))
+                if j == TOK - 1:
+                    nc.sync.dma_start(
+                        out=dram_group("v", n, b).rearrange("h (p j) d -> p h (j d)", j=TOK),
+                        in_=ov[:].rearrange("p h j d -> p h (j d)"),
+                    )
+
+            return empty
 
         for i in range(4, LOOK):
             fill(i)
         zt = None
         ot = None
+        waiting = {}
         for i in range(n_banks - TOK):
             gi, j = divmod(i, TOK)
             kind, n, b = groups[gi]
             if j == 0:
                 zt = zpool.tile([P, HEADS, TOK, 2 * D], F32, name="zt")
                 ot = opool.tile([P, HEADS, TOK, D], F32, name="ot")
-            for h in range(HEADS - 1):
+            for h in range(HEADS):
                 rotate(i, zt, h)
             if i in quantize_at:
                 quantize(quantize_at[i][0], quantize_at[i][1])
-            rotate(i, zt, HEADS - 1)
             if i + LOOK < n_banks:
                 fill(i + LOOK)
+            if i in waiting:
+                waiting[i]()
             if i in side_jobs:
                 u = side_jobs[i]
+                on_vector = u in (17, 21)
                 if u < HEADS * len(late_sets):
-                    turn_bank(late_sets[u // HEADS], u % HEADS, ps_s)
+                    empty = turn_bank(late_sets[u // HEADS], u % HEADS, ps_s, on_vector)
                 else:
-                    v_bank(u - HEADS * len(late_sets))
+                    empty = v_bank(u - HEADS * len(late_sets), on_vector)
+                if on_vector:
+                    waiting[i + 2] = empty
+                else:
+                    empty()
             if gi == len(groups) - 2:
                 if j % 2 == 1:
                     zv = zt[:, :, j - 1 : j + 1, :].rearrange("p h j (a c f) -> p h j a c f", a=2, c=2)

from contextlib import ExitStack

import concourse.mybir as mybir
from concourse.masks import make_identity

F32 = mybir.dt.float32
BF16 = mybir.dt.bfloat16
U32 = mybir.dt.uint32
U8 = mybir.dt.uint8
FP8 = mybir.dt.float8_e4m3fn
FP8X4 = mybir.dt.float8_e4m3fn_x4
ALU = mybir.AluOpType
ACT = mybir.ActivationFunctionType

P = 128
BATCH, SEQ, K = 2, 512, 1024
D = 128
HALF = D // 2
EPS = 1e-6
N_TILE = 512
HEADS = N_TILE // D
TOK = SEQ // P
PASSES = K // 512
Q_TILES, K_TILES, V_TILES = 4, 2, 2
LOOK = 6

FLOPS = 2 * BATCH * SEQ * K * (Q_TILES + K_TILES + V_TILES) * N_TILE


def tile_qwen3attention_pa_kernel(
    tc, x, cos, sin, wq_bytes, wq_scale, wk, wv, q_norm_w, k_norm_w, out_0, out_1, out_2
):
    nc = tc.nc
    outs = {"q": out_0, "k": out_1, "v": out_2}
    groups = [("q", n, b) for n in range(Q_TILES) for b in range(BATCH)] + [
        ("k", n, b) for n in range(K_TILES) for b in range(BATCH)
    ]
    n_banks = len(groups) * TOK
    late_sets = [("q", 2), ("q", 3), ("k", 0), ("k", 1)]
    quantize_at = {3: (("v", 1), None), 7: (("q", 2), None)}
    for s in (1, 2, 3):
        quantize_at[8 * s + 3] = (late_sets[s], 0)
        quantize_at[8 * s + 7] = (late_sets[s], 1)
    side_slots = [i for i in range(40) if i % 5 != 4]
    side_jobs = dict((side_slots[u], u) for u in range(len(side_slots)))

    with ExitStack() as ctx:
        ctx.enter_context(tc.manual_schedule())
        keep = ctx.enter_context(tc.tile_pool(name="keep", bufs=1))
        small = ctx.enter_context(tc.tile_pool(name="small", bufs=8))
        late = ctx.enter_context(tc.tile_pool(name="late", bufs=1))
        ps_o = ctx.enter_context(tc.psum_pool(name="ps_o", bufs=4))
        pools = {}

        zero = keep.tile([P, 1], F32, name="zero")
        nc.vector.memset(zero[:], 0.0)
        eps_t = keep.tile([P, 1], F32, name="eps_t")
        nc.vector.tensor_scalar(out=eps_t[:], in0=zero[:], scalar1=EPS, scalar2=None, op0=ALU.add)
        ident = keep.tile([P, P], F32, name="ident")
        make_identity(nc, ident[:])
        warm = keep.tile([P, 1], F32, name="warm")
        nc.scalar.activation(out=warm[:], in_=eps_t[:], func=ACT.Abs_reciprocal_sqrt)

        cs = keep.tile([P, TOK, HALF], BF16, name="cs")
        nc.sync.dma_start(out=cs[:], in_=cos[0, 0].rearrange("(p j) f -> p j f", j=TOK))
        sn = keep.tile([P, TOK, HALF], BF16, name="sn")
        nc.sync.dma_start(out=sn[:], in_=sin[0, 0].rearrange("(p j) f -> p j f", j=TOK))
        gain_q = keep.tile([P, D], BF16, name="gain_q")
        nc.sync.dma_start(out=gain_q[:], in_=q_norm_w.partition_broadcast(P))
        gain_k = keep.tile([P, D], BF16, name="gain_k")
        nc.sync.dma_start(out=gain_k[:], in_=k_norm_w.partition_broadcast(P))

        codes = {}
        planes = {}
        for key in [("x", b) for b in range(BATCH)] + [
            (kind, n)
            for kind, tiles in (("q", Q_TILES), ("k", K_TILES), ("v", V_TILES))
            for n in range(tiles)
        ]:
            codes[key] = keep.tile([P, PASSES * N_TILE], U32, name="codes_%s%d" % key, align_bytes=64)
            planes[key] = keep.tile([P, PASSES * N_TILE], U8, name="planes_%s%d" % key, align_bytes=64)

        tables = {}
        raw = {}
        grouped = {}
        banks = {}
        rstd = {}
        state = {}

        def make_table(kind, gain):
            tab = keep.tile([P, TOK, 2 * D], F32, name="tab_%s" % kind)
            tv = tab[:].rearrange("p j (a c f) -> p j a c f", a=2, c=2)
            w1 = gain[:, 0:HALF].unsqueeze(1).to_broadcast([P, TOK, HALF])
            w2 = gain[:, HALF:D].unsqueeze(1).to_broadcast([P, TOK, HALF])
            nc.vector.tensor_tensor(out=tv[:, :, 0, 0, :], in0=cs[:], in1=w1, op=ALU.mult)
            nc.vector.scalar_tensor_tensor(
                out=tv[:, :, 0, 1, :], in0=sn[:], scalar=-1.0, in1=w2, op0=ALU.mult, op1=ALU.mult
            )
            nc.vector.tensor_tensor(out=tv[:, :, 1, 0, :], in0=sn[:], in1=w1, op=ALU.mult)
            nc.vector.tensor_tensor(out=tv[:, :, 1, 1, :], in0=cs[:], in1=w2, op=ALU.mult)
            tables[kind] = tab

        def turn_bank(key, i, psum, on_vector=False):
            if i == 0:
                wg = late.tile([P, PASSES * N_TILE * 4], BF16, name="wg", bufs=4, align_bytes=64)
                grouped[key] = wg
            dst = grouped[key][:].bitcast(F32).rearrange("p (g c u) -> p g c u", g=PASSES, u=2)
            words = raw[key][:, i, :].bitcast(F32)
            tb = psum.tile([P, N_TILE], F32, name="tb")
            for g in range(PASSES):
                for u in range(2):
                    q = 2 * g + u
                    nc.tensor.transpose(
                        tb[:, q * P : (q + 1) * P], words[:, 256 * g + u : 256 * (g + 1) : 2], ident[:]
                    )
            copy = nc.vector.tensor_copy if on_vector else nc.scalar.copy
            return lambda: copy(
                out=dst[:, :, i * P : (i + 1) * P, :],
                in_=tb[:].rearrange("p (g u r) -> p g r u", g=PASSES, u=2),
            )

        def quantize(key, g=None):
            cols = slice(0, PASSES * N_TILE) if g is None else slice(g * N_TILE, (g + 1) * N_TILE)
            nc.vector.quantize_mx(
                out=codes[key][:, cols].bitcast(FP8X4),
                scales=planes[key][:, cols],
                in_=grouped[key][:, 4 * cols.start : 4 * cols.stop],
            )

        def mx_bank(bank, wkey, b, j):
            for g in range(PASSES):
                m_cols = slice(g * N_TILE + j * P, g * N_TILE + (j + 1) * P)
                n_cols = slice(g * N_TILE, (g + 1) * N_TILE)
                nc.tensor.matmul_mx(
                    out=bank[:],
                    lhsT=codes[("x", b)][:, m_cols].bitcast(FP8X4),
                    lhsT_scale=planes[("x", b)][:, m_cols],
                    rhs=codes[wkey][:, n_cols].bitcast(FP8X4),
                    rhs_scale=planes[wkey][:, n_cols],
                    start=(g == 0),
                    stop=(g == PASSES - 1),
                )

        def fill(i):
            kind, n, b = groups[i // TOK]
            if i % LOOK < 4:
                ob = ps_o.tile([P, N_TILE], F32, name="ob")
            else:
                ob = pools["ps_o2"].tile([P, N_TILE], F32, name="ob2")
            mx_bank(ob, (kind, n), b, i % TOK)
            banks[i] = ob
            odd = i % 2
            if odd == 0:
                ss = small.tile([P, 2 * HEADS], F32, name="ss")
                state["ss"] = ss
            ss = state["ss"]
            for h in range(HEADS):
                junk = small.tile([P, D], BF16, name="junk")
                col = odd * HEADS + h
                nc.scalar.activation(
                    out=junk[:], in_=ob[:, h * D : (h + 1) * D], func=ACT.Square, accum_out=ss[:, col : col + 1]
                )
            if odd == 1:
                rr = small.tile([P, 2 * HEADS], F32, name="rr")
                nc.scalar.activation(
                    out=rr[:], in_=ss[:], func=ACT.Abs_reciprocal_sqrt, bias=eps_t[:, 0:1], scale=1.0 / D
                )
                rstd[i - 1] = rr
                rstd[i] = rr

        with tc.psum_pool(name="ps_t", bufs=4) as ps_t, tc.tile_pool(name="stage", bufs=1) as stage:
            scale_bc = stage.tile([P, K], F32, name="scale_bc")
            nc.sync.dma_start(out=scale_bc[:], in_=wq_scale.rearrange("o k -> (o k)").partition_broadcast(P))
            wq_in = {}

            def load_bytes(n, pieces):
                wq_codes_in = stage.tile([P, HEADS, K], U8, name="wq_codes_in%d" % n)
                rows = wq_bytes[n * N_TILE : (n + 1) * N_TILE, :].rearrange("(i r) k -> r i k", r=P)
                step = HEADS // pieces
                for i in range(0, HEADS, step):
                    nc.sync.dma_start(out=wq_codes_in[:, i : i + step, :], in_=rows[:, i : i + step, :])
                wq_in[n] = wq_codes_in

            def load_x(b):
                t = stage.tile([P, TOK, K], BF16, name="raw_x%d" % b)
                nc.sync.dma_start(out=t[:], in_=x[b].rearrange("(p j) k -> p j k", j=TOK))
                raw[("x", b)] = t

            def load_w(kind, w, n):
                pool = late if (kind, n) in late_sets else stage
                t = pool.tile([P, HEADS, K], BF16, name="raw_%s%d" % (kind, n))
                nc.sync.dma_start(out=t[:], in_=w[n * N_TILE : (n + 1) * N_TILE, :].rearrange("(i r) k -> r i k", r=P))
                raw[(kind, n)] = t

            def widen(n):
                if ("q", n) in late_sets:
                    wide = late.tile([P, HEADS, K], BF16, name="wide%d" % n)
                else:
                    wide = stage.tile([P, HEADS, K], BF16, name="wide%d" % n)
                for i in range(HEADS):
                    nc.vector.tensor_tensor(
                        out=wide[:, i, :], in0=wq_in[n][:, i, :].bitcast(FP8), in1=scale_bc[:], op=ALU.mult
                    )
                raw[("q", n)] = wide

            def turn(key):
                for i in range(HEADS):
                    turn_bank(key, i, ps_t)()

            load_bytes(0, 2)
            load_x(0)
            load_bytes(1, 1)
            load_x(1)
            load_w("v", wv, 0)
            load_bytes(2, 1)
            load_w("v", wv, 1)
            load_bytes(3, 1)
            load_w("k", wk, 0)
            load_w("k", wk, 1)

            make_table("q", gain_q)
            make_table("k", gain_k)
            widen(0)
            turn(("x", 0))
            turn(("q", 0))
            widen(1)
            quantize(("x", 0))
            widen(2)
            turn(("x", 1))
            turn(("q", 1))
            turn(("v", 0))
            quantize(("q", 0))
            for i in range(4):
                fill(i)
            turn(("v", 1))
            quantize(("x", 1))
            widen(3)
            quantize(("q", 1))
            quantize(("v", 0))

        pools["ps_o2"] = ctx.enter_context(tc.psum_pool(name="ps_o2", bufs=LOOK - 4))
        ps_s = ctx.enter_context(tc.psum_pool(name="ps_s", bufs=2))
        zpool = ctx.enter_context(tc.tile_pool(name="zpool", bufs=3))
        opool = ctx.enter_context(tc.tile_pool(name="opool", bufs=3))

        def dram_group(kind, n, b):
            return outs[kind][b, n * HEADS : (n + 1) * HEADS]

        def rotate(i, zt, h):
            kind = groups[i // TOK][0]
            j = i % TOK
            col = (i % 2) * HEADS + h
            nc.vector.scalar_tensor_tensor(
                out=zt[:, h, j, :].rearrange("p (a d) -> p a d", a=2),
                in0=banks[i][:, h * D : (h + 1) * D].unsqueeze(1).to_broadcast([P, 2, D]),
                scalar=rstd[i][:, col : col + 1],
                in1=tables[kind][:, j, :].rearrange("p (a d) -> p a d", a=2),
                op0=ALU.mult,
                op1=ALU.mult,
            )

        def v_bank(k, on_vector):
            n, b, j = k // (BATCH * TOK), (k // TOK) % BATCH, k % TOK
            vb = ps_s.tile([P, N_TILE], F32, name="tb")
            mx_bank(vb, ("v", n), b, j)
            if j == 0:
                ov = opool.tile([P, HEADS, TOK, D], F32, name="ov", bufs=2)
                state["ov"] = ov
            ov = state["ov"]
            copy = nc.vector.tensor_copy if on_vector else nc.scalar.copy

            def empty():
                copy(out=ov[:, :, j, :], in_=vb[:].rearrange("p (h d) -> p h d", h=HEADS))
                if j == TOK - 1:
                    nc.sync.dma_start(
                        out=dram_group("v", n, b).rearrange("h (p j) d -> p h (j d)", j=TOK),
                        in_=ov[:].rearrange("p h j d -> p h (j d)"),
                    )

            return empty

        for i in range(4, LOOK):
            fill(i)
        zt = None
        ot = None
        waiting = {}
        for i in range(n_banks - TOK):
            gi, j = divmod(i, TOK)
            kind, n, b = groups[gi]
            if j == 0:
                zt = zpool.tile([P, HEADS, TOK, 2 * D], F32, name="zt")
                ot = opool.tile([P, HEADS, TOK, D], F32, name="ot")
            for h in range(HEADS):
                rotate(i, zt, h)
            if i in quantize_at:
                quantize(quantize_at[i][0], quantize_at[i][1])
            if i + LOOK < n_banks:
                fill(i + LOOK)
            if i in waiting:
                waiting[i]()
            if i in side_jobs:
                u = side_jobs[i]
                on_vector = u in (17, 21)
                if u < HEADS * len(late_sets):
                    empty = turn_bank(late_sets[u // HEADS], u % HEADS, ps_s, on_vector)
                else:
                    empty = v_bank(u - HEADS * len(late_sets), on_vector)
                if on_vector:
                    waiting[i + 2] = empty
                else:
                    empty()
            if gi == len(groups) - 2:
                if j % 2 == 1:
                    zv = zt[:, :, j - 1 : j + 1, :].rearrange("p h j (a c f) -> p h j a c f", a=2, c=2)
                    nc.gpsimd.tensor_tensor(
                        out=ot[:, :, j - 1 : j + 1, :].rearrange("p h j (a f) -> p h j a f", a=2),
                        in0=zv[:, :, :, :, 0, :],
                        in1=zv[:, :, :, :, 1, :],
                        op=ALU.add,
                    )
                    nc.sync.dma_start(
                        out=dram_group(kind, n, b).rearrange("h (p j) d -> p h j d", j=TOK)[:, :, j - 1 : j + 1, :],
                        in_=ot[:, :, j - 1 : j + 1, :],
                    )
            elif j == TOK - 1:
                zv = zt[:].rearrange("p h j (a c f) -> p (h j) a c f", a=2, c=2)
                nc.gpsimd.tensor_tensor(
                    out=ot[:].rearrange("p h j (a f) -> p (h j) a f", a=2),
                    in0=zv[:, :, :, 0, :],
                    in1=zv[:, :, :, 1, :],
                    op=ALU.add,
                )
                nc.sync.dma_start(
                    out=dram_group(kind, n, b).rearrange("h (p j) d -> p h (j d)", j=TOK),
                    in_=ot[:].rearrange("p h j d -> p h (j d)"),
                )

        kind, n, b = groups[-1]
        first = n_banks - TOK
        zt = zpool.tile([P, HEADS, TOK, 2 * D], F32, name="zt")
        ot = opool.tile([P, HEADS, TOK, D], F32, name="ot")

        def add_head(h):
            zv = zt[:, h, :, :].rearrange("p j (a c f) -> p j a c f", a=2, c=2)
            nc.vector.tensor_tensor(
                out=ot[:, h, :, :].rearrange("p j (a f) -> p j a f", a=2),
                in0=zv[:, :, :, 0, :],
                in1=zv[:, :, :, 1, :],
                op=ALU.add,
            )
            nc.scalar.dma_start(
                out=dram_group(kind, n, b)[h].rearrange("(p j) d -> p (j d)", j=TOK),
                in_=ot[:, h, :, :].rearrange("p j d -> p (j d)"),
            )

        for h in range(HEADS):
            for jj in range(TOK):
                rotate(first + jj, zt, h)
            if h == HEADS - 2:
                add_head(0)
        for h in range(1, HEADS):
            add_head(h)
